import numpy as np
import ml_dtypes


def mxq(x, axis, fmt="e4m3"):
    dtype, down = {"e4m3": (ml_dtypes.float8_e4m3fn, 7), "e5m2": (ml_dtypes.float8_e5m2, 14)}[fmt]
    v = np.moveaxis(np.asarray(x, np.float32).astype(ml_dtypes.bfloat16).astype(np.float64), axis, -1)
    blocks = v.reshape(v.shape[:-1] + (-1, 32))
    amax = np.abs(blocks).max(-1, keepdims=True)
    byte = np.maximum(np.where(amax > 0, np.frexp(amax)[1] - 1 + 127, 0) - down, 1)
    scale = np.exp2(byte - 127.0)
    codes = (blocks / scale).astype(np.float32).astype(dtype).astype(np.float64)
    return np.moveaxis((codes * scale).reshape(v.shape), -1, axis)


WIDE = False


def mx_kscale(k):
    if not WIDE:
        return np.ones(k)
    levels = np.array([30, -30])
    if k % 512:
        return np.exp2(np.random.permutation(np.resize(levels, k // 32))).repeat(32)
    a = np.empty((k // 512, 16))
    for p in range(k // 512):
        a[p, :8] = np.random.permutation(np.resize(levels, 8))
        for g in range(8):
            far = levels[np.abs(levels - a[p, g]) >= 10]
            a[p, g + 8] = far[np.random.randint(len(far))]
    return np.exp2(a.ravel()).repeat(32)


BF16 = ml_dtypes.bfloat16


def bf(x):
    return np.asarray(x, np.float32).astype(BF16)


def f64(x):
    return np.asarray(x).astype(np.float64)


B, T, C, H, G, D = 1, 512, 2048, 16, 4, 128
EPS = 1e-6
HALF = D // 2


def rmsnorm(u, w):
    rms = np.sqrt((u * u).sum(-1, keepdims=True)) / np.sqrt(D)
    return w * (u / (rms + EPS))


def rope(u, cos, sin):
    u1, u2 = u[..., :HALF], u[..., HALF:]
    c = cos[None, :, None, :]
    s = sin[None, :, None, :]
    return np.concatenate([u1 * c + u2 * s, -u1 * s + u2 * c], axis=-1)


def setup_inputs():
    s = mx_kscale(C)
    a = 1.0 / np.sqrt(C)
    ang = np.outer(np.arange(T), 1.0 / (10000.0 ** (np.arange(0, D, 2) / D)))
    return {"x": bf(np.random.standard_normal((B, T, C)) * s),
            "Wq": bf(np.random.standard_normal((H * D, C)) * a / s),
            "Wk": bf(np.random.standard_normal((G * D, C)) * a / s),
            "Wv": bf(np.random.standard_normal((G * D, C)) * a / s),
            "q_norm_w": bf(1.0 + 0.1 * np.random.standard_normal(D)),
            "k_norm_w": bf(1.0 + 0.1 * np.random.standard_normal(D)),
            "rope_cos": bf(np.cos(ang)),
            "rope_sin": bf(np.sin(ang))}


def reference(x, Wq, Wk, Wv, q_norm_w, k_norm_w, rope_cos, rope_sin):
    xq = mxq(f64(x), 2, "e5m2")
    q = (xq @ mxq(f64(Wq), 1, "e5m2").T).reshape(B, T, H, D)
    k = (xq @ mxq(f64(Wk), 1, "e5m2").T).reshape(B, T, G, D)
    v = (xq @ mxq(f64(Wv), 1, "e5m2").T).reshape(B, T, G, D)
    cos, sin = f64(rope_cos), f64(rope_sin)
    q = rope(rmsnorm(q, f64(q_norm_w)), cos, sin)
    k = rope(rmsnorm(k, f64(k_norm_w)), cos, sin)
    return q, k, v

@@ -1,0 +1,263 @@
+from contextlib import ExitStack
+
+import concourse.mybir as mybir
+from concourse.masks import make_identity
+
+T, C, D = 512, 2048, 128
+HALF = D // 2
+EPS = 1e-6
+FLOPS = 2 * T * C * (2048 + 512 + 512)
+
+F32 = mybir.dt.float32
+BF16 = mybir.dt.bfloat16
+U32 = mybir.dt.uint32
+U8 = mybir.dt.uint8
+E5M2X4 = mybir.dt.float8_e5m2_x4
+ACT = mybir.ActivationFunctionType
+ALU = mybir.AluOpType
+
+P = 128
+N = 512
+PASSES = 4
+WORDS = 256
+TOKEN_TILES = 4
+HEADS = 4
+CHUNKS = 6
+K_CHUNK, V_CHUNK = 4, 5
+
+
+def tile_groupedqueryattention_pa_kernel(
+    tc, x, Wq, Wk, Wv, q_norm_w, k_norm_w, rope_cos, rope_sin, out_0, out_1, out_2
+):
+    nc = tc.nc
+    x_rows = x[0].rearrange("(p m) k -> p m k", m=TOKEN_TILES)
+    w_rows = [Wq[c * N:(c + 1) * N, :] for c in range(4)] + [Wk, Wv]
+    w_rows = [w.rearrange("(r p) k -> p r k", p=P) for w in w_rows]
+    q_out = out_0[0].rearrange("(p m) h d -> p m (h d)", m=TOKEN_TILES)
+    k_out = out_1[0].rearrange("(p m) h d -> p m (h d)", m=TOKEN_TILES)
+    v_out = out_2[0].rearrange("(p m) h d -> p m (h d)", m=TOKEN_TILES)
+
+    def out_rows(c, m):
+        if c == K_CHUNK:
+            return k_out[:, m, :]
+        if c == V_CHUNK:
+            return v_out[:, m, :]
+        return q_out[:, m, c * N:(c + 1) * N]
+
+    with ExitStack() as ctx:
+        keep = ctx.enter_context(tc.tile_pool(name="keep", bufs=1))
+        work = ctx.enter_context(tc.tile_pool(name="work", bufs=1))
+        psum = ctx.enter_context(tc.psum_pool(name="psum", bufs=4))
+        ctx.enter_context(tc.manual_schedule())
+
+        ident = keep.tile([P, P], F32, name="ident")
+        make_identity(nc, ident[:])
+
+        slots = {}
+
+        def load_x(m, pieces):
+            slots[("x", m)] = []
+            width = C // pieces
+            for i in range(pieces):
+                raw = keep.tile([P, width], BF16, name="x_raw_%d_%d" % (m, i))
+                nc.sync.dma_start(out=raw[:], in_=x_rows[:, m, i * width:(i + 1) * width])
+                words = raw[:].bitcast(F32)
+                for g in range(PASSES // pieces):
+                    slots[("x", m)].append(words[:, g * WORDS:(g + 1) * WORDS])
+
+        def load_w(c, g0, count):
+            raw = keep.tile([P, 4, count * 512], BF16, name="w_raw_%d_%d" % (c, g0))
+            nc.sync.dma_start(out=raw[:], in_=w_rows[c][:, :, g0 * 512:(g0 + count) * 512])
+            words = raw[:].bitcast(F32)
+            for j in range(count):
+                slots[("w", c, g0 + j)] = [words[:, r, j * WORDS:(j + 1) * WORDS] for r in range(4)]
+
+        load_x(0, 2)
+        for g in range(PASSES):
+            load_w(0, g, 1)
+        load_x(1, 1)
+        load_x(2, 1)
+        load_w(1, 0, 2)
+        load_x(3, 1)
+        load_w(1, 2, 2)
+        for c in range(2, CHUNKS):
+            load_w(c, 0, 2)
+            load_w(c, 2, 2)
+
+        gains = keep.tile([P, 2 * D], BF16, name="gains")
+        ones = keep.tile([P, P], BF16, name="ones")
+        nc.vector.memset(gains[:], 0.0)
+        nc.vector.memset(ones[:], 1.0)
+        cos = keep.tile([P, TOKEN_TILES, HALF], BF16, name="cos")
+        sin = keep.tile([P, TOKEN_TILES, HALF], BF16, name="sin")
+        nc.gpsimd.dma_start(out=gains[0:1, 0:D], in_=q_norm_w.unsqueeze(0))
+        nc.gpsimd.dma_start(out=gains[0:1, D:2 * D], in_=k_norm_w.unsqueeze(0))
+        nc.gpsimd.dma_start(out=cos[:], in_=rope_cos.rearrange("(p m) i -> p m i", m=TOKEN_TILES))
+        nc.gpsimd.dma_start(out=sin[:], in_=rope_sin.rearrange("(p m) i -> p m i", m=TOKEN_TILES))
+
+        tables = [keep.tile([P, TOKEN_TILES, 2, D], F32, name="table_%d" % i) for i in range(2)]
+
+        def build_tables():
+            spread = psum.tile([P, 2 * D], F32, name="spread", tag="acc")
+            nc.tensor.matmul(spread[:], lhsT=ones[:], rhs=gains[:], start=True, stop=True)
+            for i in range(2):
+                gain = spread[:, i * D:(i + 1) * D]
+                shape = [P, TOKEN_TILES, 2, HALF]
+                nc.vector.tensor_tensor(
+                    out=tables[i][:, :, 0, :].rearrange("p m (a i) -> p m a i", a=2),
+                    in0=gain.rearrange("p (a i) -> p a i", a=2).unsqueeze(1).to_broadcast(shape),
+                    in1=cos[:].unsqueeze(2).to_broadcast(shape),
+                    op=ALU.mult,
+                )
+                shape = [P, TOKEN_TILES, HALF]
+                nc.vector.scalar_tensor_tensor(
+                    out=tables[i][:, :, 1, 0:HALF],
+                    in0=gain[:, 0:HALF].unsqueeze(1).to_broadcast(shape),
+                    scalar=-1.0,
+                    in1=sin[:],
+                    op0=ALU.mult,
+                    op1=ALU.mult,
+                )
+                nc.vector.tensor_tensor(
+                    out=tables[i][:, :, 1, HALF:D],
+                    in0=gain[:, HALF:D].unsqueeze(1).to_broadcast(shape),
+                    in1=sin[:],
+                    op=ALU.mult,
+                )
+
+        codes, scales, staged, banks = {}, {}, {}, {}
+
+        def transpose(unit):
+            banks[unit] = []
+            for b in range(2):
+                bank = psum.tile([P, 2, 2, P], F32, name="bank", tag="turn")
+                for s in range(2):
+                    for u in range(2):
+                        nc.tensor.transpose(bank[:, s, u, :], slots[unit][2 * b + s][:, u:WORDS:2], ident[:])
+                banks[unit].append(bank)
+
+        def empty_bank(unit, b):
+            if b == 0:
+                staged[unit] = work.tile([P, 4 * N], BF16, name="staged", bufs=4, align_bytes=64)
+            words = staged[unit][:].bitcast(F32)[:, b * N:(b + 1) * N]
+            nc.scalar.copy(
+                out=words.rearrange("p (s n u) -> p s n u", s=2, u=2),
+                in_=banks[unit][b][:].rearrange("p s u n -> p s n u"),
+            )
+
+        def quantize(unit):
+            depth = TOKEN_TILES if unit[0] == "x" else 2 * PASSES
+            codes[unit] = work.tile([P, N], U32, name=unit[0] + "_codes", bufs=depth, align_bytes=64)
+            scales[unit] = work.tile([P, N], U8, name=unit[0] + "_scales", bufs=depth, align_bytes=64)
+            nc.vector.quantize_mx(out=codes[unit][:].bitcast(E5M2X4), scales=scales[unit][:], in_=staged[unit][:])
+
+        acc, sums, rms, inv, terms = {}, {}, {}, {}, {}
+
+        def multiply(group):
+            c, m = group
+            acc[group] = psum.tile([P, N], F32, name="acc", tag="acc")
+            for g in range(PASSES):
+                cols = slice(g * P, (g + 1) * P)
+                nc.tensor.matmul_mx(
+                    out=acc[group][:],
+                    lhsT=codes[("x", m)][:, cols].bitcast(E5M2X4),
+                    lhsT_scale=scales[("x", m)][:, cols],
+                    rhs=codes[("w", c, g)][:].bitcast(E5M2X4),
+                    rhs_scale=scales[("w", c, g)][:],
+                    start=(g == 0),
+                    stop=(g == PASSES - 1),
+                )
+
+        def normed(group):
+            return group is not None and group[0] != V_CHUNK
+
+        def sum_squares(group):
+            squares = work.tile([P, N], BF16, name="squares", bufs=2)
+            sums[group] = work.tile([P, HEADS], F32, name="sums", bufs=3)
+            for h in range(HEADS):
+                cols = slice(h * D, (h + 1) * D)
+                nc.scalar.activation(
+                    out=squares[:, cols], in_=acc[group][:, cols], func=ACT.Square,
+                    accum_out=sums[group][:, h:h + 1],
+                )
+
+        def root(group):
+            rms[group] = work.tile([P, HEADS], F32, name="rms", bufs=3)
+            nc.scalar.activation(out=rms[group][:], in_=sums[group][:], func=ACT.Sqrt, scale=1.0 / D)
+
+        def add_eps(group):
+            nc.scalar.activation(out=sums[group][:], in_=rms[group][:], func=ACT.Copy, bias=EPS)
+
+        def invert(group):
+            inv[group] = work.tile([P, HEADS], F32, name="inv", bufs=3)
+            nc.vector.reciprocal(out=inv[group][:], in_=sums[group][:])
+
+        def products(group):
+            c, m = group
+            table = tables[1 if c == K_CHUNK else 0]
+            terms[group] = work.tile([P, HEADS, 2, D], F32, name="terms", bufs=3)
+            for h in range(HEADS):
+                nc.vector.scalar_tensor_tensor(
+                    out=terms[group][:, h, :, :],
+                    in0=acc[group][:, h * D:(h + 1) * D].unsqueeze(1).to_broadcast([P, 2, D]),
+                    scalar=inv[group][:, h:h + 1],
+                    in1=table[:, m, :, :],
+                    op0=ALU.mult,
+                    op1=ALU.mult,
+                )
+
+        def rotate_and_store(group):
+            result = work.tile([P, HEADS, D], F32, name="result", bufs=12)
+            for lo, other in ((0, HALF), (HALF, 0)):
+                nc.vector.tensor_tensor(
+                    out=result[:, :, lo:lo + HALF],
+                    in0=terms[group][:, :, 0, lo:lo + HALF],
+                    in1=terms[group][:, :, 1, other:other + HALF],
+                    op=ALU.add,
+                )
+            nc.sync.dma_start(out=out_rows(*group), in_=result[:].rearrange("p h d -> p (h d)"))
+
+        def copy_and_store(group):
+            result = work.tile([P, N], F32, name="result", bufs=12)
+            nc.scalar.copy(out=result[:], in_=acc[group][:])
+            nc.sync.dma_start(out=out_rows(*group), in_=result[:])
+
+        units = [("x", 0)] + [("w", 0, g) for g in range(PASSES)] + [("x", 1)]
+        units += [("x", 2), ("w", 1, 0), ("x", 3), ("w", 1, 1), ("w", 1, 2), ("w", 1, 3)]
+        units += [("w", c, g) for c in range(2, CHUNKS) for g in range(PASSES)]
+        groups = [(c, m) for c in range(CHUNKS) for m in range(TOKEN_TILES)]
+        counts = [6, 2, 2, 2] + [1] * 16 + [0] * 6
+
+        done = 0
+        for step in range(len(groups) + 2):
+            mine = units[done:done + counts[step]]
+            done += counts[step]
+            last = groups[step - 1] if 1 <= step <= len(groups) else None
+            before = groups[step - 2] if step >= 2 else None
+
+            small = []
+            if normed(last):
+                sum_squares(last)
+                small = [root, add_eps]
+            elif last is not None:
+                copy_and_store(last)
+            for i, unit in enumerate(mine):
+                transpose(unit)
+                for b in range(2):
+                    empty_bank(unit, b)
+                    if small:
+                        small[0](last)
+                        small = small[1:]
+                quantize(unit)
+                if step == 0 and i == 3:
+                    build_tables()
+            for call in small:
+                call(last)
+            if step < len(groups):
+                multiply(groups[step])
+            if normed(last):
+                invert(last)
+            if normed(before):
+                rotate_and_store(before)
+            if normed(last):
+                products(last)

@@ -76,6 +76,17 @@ def tile_groupedqueryattention_pa_kernel(
         for g in range(PASSES):
             load_w(0, g, 1)
         load_x(1, 1)
+        gains = keep.tile([P, 2 * D], BF16, name="gains")
+        ones = keep.tile([P, P], BF16, name="ones")
+        nc.vector.memset(gains[:], 0.0)
+        nc.vector.memset(ones[:], 1.0)
+        cos = keep.tile([P, TOKEN_TILES, HALF], BF16, name="cos")
+        sin = keep.tile([P, TOKEN_TILES, HALF], BF16, name="sin")
+        nc.sync.dma_start(out=gains[0:1, 0:D], in_=q_norm_w.unsqueeze(0))
+        nc.sync.dma_start(out=gains[0:1, D:2 * D], in_=k_norm_w.unsqueeze(0))
+        nc.sync.dma_start(out=cos[:], in_=rope_cos.rearrange("(p m) i -> p m i", m=TOKEN_TILES))
+        nc.sync.dma_start(out=sin[:], in_=rope_sin.rearrange("(p m) i -> p m i", m=TOKEN_TILES))
+
         load_x(2, 1)
         load_w(1, 0, 2)
         load_x(3, 1)
@@ -83,17 +94,6 @@ def tile_groupedqueryattention_pa_kernel(
         for c in range(2, CHUNKS):
             load_w(c, 0, 2)
             load_w(c, 2, 2)
-
-        gains = keep.tile([P, 2 * D], BF16, name="gains")
-        ones = keep.tile([P, P], BF16, name="ones")
-        nc.vector.memset(gains[:], 0.0)
-        nc.vector.memset(ones[:], 1.0)
-        cos = keep.tile([P, TOKEN_TILES, HALF], BF16, name="cos")
-        sin = keep.tile([P, TOKEN_TILES, HALF], BF16, name="sin")
-        nc.gpsimd.dma_start(out=gains[0:1, 0:D], in_=q_norm_w.unsqueeze(0))
-        nc.gpsimd.dma_start(out=gains[0:1, D:2 * D], in_=k_norm_w.unsqueeze(0))
-        nc.gpsimd.dma_start(out=cos[:], in_=rope_cos.rearrange("(p m) i -> p m i", m=TOKEN_TILES))
-        nc.gpsimd.dma_start(out=sin[:], in_=rope_sin.rearrange("(p m) i -> p m i", m=TOKEN_TILES))
 
         tables = [keep.tile([P, TOKEN_TILES, 2, D], F32, name="table_%d" % i) for i in range(2)]
 
@@ -151,11 +151,11 @@ def tile_groupedqueryattention_pa_kernel(
             scales[unit] = work.tile([P, N], U8, name=unit[0] + "_scales", bufs=depth, align_bytes=64)
             nc.vector.quantize_mx(out=codes[unit][:].bitcast(E5M2X4), scales=scales[unit][:], in_=staged[unit][:])
 
-        acc, sums, rms, inv, terms = {}, {}, {}, {}, {}
+        acc, stat, terms = {}, {}, {}
 
         def multiply(group):
             c, m = group
-            acc[group] = psum.tile([P, N], F32, name="acc", tag="acc")
+            acc[group] = psum.tile([P, N], F32, name="acc", tag="turn" if c == V_CHUNK else "acc")
             for g in range(PASSES):
                 cols = slice(g * P, (g + 1) * P)
                 nc.tensor.matmul_mx(
@@ -168,29 +168,30 @@ def tile_groupedqueryattention_pa_kernel(
                     stop=(g == PASSES - 1),
                 )
 
-        def normed(group):
-            return group is not None and group[0] != V_CHUNK
-
         def sum_squares(group):
+            stat[group] = work.tile([P, HEADS], F32, name="sums", bufs=3)
             squares = work.tile([P, N], BF16, name="squares", bufs=2)
-            sums[group] = work.tile([P, HEADS], F32, name="sums", bufs=3)
             for h in range(HEADS):
                 cols = slice(h * D, (h + 1) * D)
                 nc.scalar.activation(
                     out=squares[:, cols], in_=acc[group][:, cols], func=ACT.Square,
-                    accum_out=sums[group][:, h:h + 1],
+                    accum_out=stat[group][:, h:h + 1],
                 )
 
         def root(group):
-            rms[group] = work.tile([P, HEADS], F32, name="rms", bufs=3)
-            nc.scalar.activation(out=rms[group][:], in_=sums[group][:], func=ACT.Sqrt, scale=1.0 / D)
+            rms = work.tile([P, HEADS], F32, name="rms", bufs=3)
+            nc.scalar.activation(out=rms[:], in_=stat[group][:], func=ACT.Sqrt, scale=1.0 / D)
+            stat[group] = rms
 
         def add_eps(group):
-            nc.scalar.activation(out=sums[group][:], in_=rms[group][:], func=ACT.Copy, bias=EPS)
+            padded = work.tile([P, HEADS], F32, name="padded", bufs=3)
+            nc.scalar.activation(out=padded[:], in_=stat[group][:], func=ACT.Copy, bias=EPS)
+            stat[group] = padded
 
         def invert(group):
-            inv[group] = work.tile([P, HEADS], F32, name="inv", bufs=3)
-            nc.vector.reciprocal(out=inv[group][:], in_=sums[group][:])
+            inverse = work.tile([P, HEADS], F32, name="inverse", bufs=3)
+            nc.vector.reciprocal(out=inverse[:], in_=stat[group][:])
+            stat[group] = inverse
 
         def products(group):
             c, m = group
@@ -200,7 +201,7 @@ def tile_groupedqueryattention_pa_kernel(
                 nc.vector.scalar_tensor_tensor(
                     out=terms[group][:, h, :, :],
                     in0=acc[group][:, h * D:(h + 1) * D].unsqueeze(1).to_broadcast([P, 2, D]),
-                    scalar=inv[group][:, h:h + 1],
+                    scalar=stat[group][:, h:h + 1],
                     in1=table[:, m, :, :],
                     op0=ALU.mult,
                     op1=ALU.mult,
@@ -222,42 +223,72 @@ def tile_groupedqueryattention_pa_kernel(
             nc.scalar.copy(out=result[:], in_=acc[group][:])
             nc.sync.dma_start(out=out_rows(*group), in_=result[:])
 
-        units = [("x", 0)] + [("w", 0, g) for g in range(PASSES)] + [("x", 1)]
-        units += [("x", 2), ("w", 1, 0), ("x", 3), ("w", 1, 1), ("w", 1, 2), ("w", 1, 3)]
-        units += [("w", c, g) for c in range(2, CHUNKS) for g in range(PASSES)]
-        groups = [(c, m) for c in range(CHUNKS) for m in range(TOKEN_TILES)]
-        counts = [6, 2, 2, 2] + [1] * 16 + [0] * 6
+        for g in range(-1, PASSES):
+            unit = ("x", 0) if g < 0 else ("w", 0, g)
+            transpose(unit)
+            empty_bank(unit, 0)
+            empty_bank(unit, 1)
+            quantize(unit)
 
-        done = 0
-        for step in range(len(groups) + 2):
-            mine = units[done:done + counts[step]]
-            done += counts[step]
-            last = groups[step - 1] if 1 <= step <= len(groups) else None
-            before = groups[step - 2] if step >= 2 else None
+        steps = [([("x", 1)], [(0, 0)])]
+        steps += [([("x", 2), ("w", 1, 0)], [(0, 1)])]
+        steps += [([("x", 3), ("w", 1, 1)], [(0, 2)])]
+        steps += [([("w", 1, 2), ("w", 1, 3)], [(0, 3)])]
+        for c in range(1, V_CHUNK):
+            for i in range(0, 4, 2):
+                steps += [([("w", c + 1, i + j) for j in range(2)], [(c, i + j) for j in range(2)])]
 
-            small = []
-            if normed(last):
-                sum_squares(last)
-                small = [root, add_eps]
-            elif last is not None:
-                copy_and_store(last)
-            for i, unit in enumerate(mine):
+        batch, waiting = [], []
+
+        def finish(group):
+            invert(group)
+            for earlier in waiting:
+                rotate_and_store(earlier)
+            waiting.clear()
+            products(group)
+            waiting.append(group)
+
+        for number, (units, groups) in enumerate(steps):
+            for unit in units:
                 transpose(unit)
-                for b in range(2):
-                    empty_bank(unit, b)
-                    if small:
-                        small[0](last)
-                        small = small[1:]
+            for group in batch[:-1]:
+                sum_squares(group)
+                root(group)
+                add_eps(group)
+            copies = [(unit, b) for unit in units for b in range(2)]
+            for group in batch[-1:]:
+                sum_squares(group)
+                empty_bank(*copies[0])
+                root(group)
+                empty_bank(*copies[1])
+                add_eps(group)
+                copies = copies[2:]
+            for unit, b in copies:
+                empty_bank(unit, b)
+
+            for group in batch[:-1]:
+                finish(group)
+            quantize(units[0])
+            for group in batch[-1:]:
+                finish(group)
+            for unit in units[1:]:
                 quantize(unit)
-                if step == 0 and i == 3:
-                    build_tables()
-            for call in small:
-                call(last)
-            if step < len(groups):
-                multiply(groups[step])
-            if normed(last):
-                invert(last)
-            if normed(before):
-                rotate_and_store(before)
-            if normed(last):
-                products(last)
+
+            for group in groups:
+                multiply(group)
+            if number == 0:
+                build_tables()
+            batch = groups
+
+        values = [(V_CHUNK, m) for m in range(TOKEN_TILES)]
+        for group in values:
+            multiply(group)
+        for group in batch:
+            sum_squares(group)
+            root(group)
+            add_eps(group)
+            finish(group)
+        for group in values[:-1]:
+            copy_and_store(group)
+        rotate_and_store(waiting[0])
+        copy_and_store(values[-1])

@@ -53,23 +53,24 @@ def tile_groupedqueryattention_pa_kernel(
         ident = keep.tile([P, P], F32, name="ident")
         make_identity(nc, ident[:])
 
-        slots = {}
+        slots, packed, sorted_words = {}, {}, {}
 
         def load_x(m, pieces):
             slots[("x", m)] = []
             width = C // pieces
             for i in range(pieces):
-                raw = keep.tile([P, width], BF16, name="x_raw_%d_%d" % (m, i))
+                raw = keep.tile([P, width], BF16, name="x_raw_%d_%d" % (m, i), align_bytes=256)
                 nc.sync.dma_start(out=raw[:], in_=x_rows[:, m, i * width:(i + 1) * width])
                 words = raw[:].bitcast(F32)
                 for g in range(PASSES // pieces):
                     slots[("x", m)].append(words[:, g * WORDS:(g + 1) * WORDS])
 
         def load_w(c, g0, count):
-            raw = keep.tile([P, 4, count * 512], BF16, name="w_raw_%d_%d" % (c, g0))
+            raw = work.tile([P, 4, count * 512], BF16, name="w_raw_%d" % count, bufs=5 if count == 2 else 4, align_bytes=256)
             nc.sync.dma_start(out=raw[:], in_=w_rows[c][:, :, g0 * 512:(g0 + count) * 512])
             words = raw[:].bitcast(F32)
             for j in range(count):
+                packed[("w", c, g0 + j)] = words[:, :, j * WORDS:(j + 1) * WORDS]
                 slots[("w", c, g0 + j)] = [words[:, r, j * WORDS:(j + 1) * WORDS] for r in range(4)]
 
         load_x(0, 2)
@@ -91,9 +92,7 @@ def tile_groupedqueryattention_pa_kernel(
         load_w(1, 0, 2)
         load_x(3, 1)
         load_w(1, 2, 2)
-        for c in range(2, CHUNKS):
-            load_w(c, 0, 2)
-            load_w(c, 2, 2)
+        later = [(c, g) for c in range(2, CHUNKS) for g in (0, 2)]
 
         tables = [keep.tile([P, TOKEN_TILES, 2, D], F32, name="table_%d" % i) for i in range(2)]
 
@@ -127,18 +126,28 @@ def tile_groupedqueryattention_pa_kernel(
 
         codes, scales, staged, banks = {}, {}, {}, {}
 
+        def sort_words(unit):
+            sorted_words[unit] = work.tile([P, 2, 2, P], F32, name="sorted_words", bufs=3, align_bytes=256)
+            nc.vector.tensor_copy(
+                out=sorted_words[unit][:], in_=packed[unit][:, 4 - 2:4, :].rearrange("p r (w u) -> p r u w", u=2)
+            )
+
         def transpose(unit):
             banks[unit] = []
             for b in range(2):
                 bank = psum.tile([P, 2, 2, P], F32, name="bank", tag="turn")
                 for s in range(2):
                     for u in range(2):
-                        nc.tensor.transpose(bank[:, s, u, :], slots[unit][2 * b + s][:, u:WORDS:2], ident[:])
+                        if unit in sorted_words and 2 * b + s >= 4 - 2:
+                            source = sorted_words[unit][:, 2 * b + s - (4 - 2), u, :]
+                        else:
+                            source = slots[unit][2 * b + s][:, u:WORDS:2]
+                        nc.tensor.transpose(bank[:, s, u, :], source, ident[:])
                 banks[unit].append(bank)
 
         def empty_bank(unit, b):
             if b == 0:
-                staged[unit] = work.tile([P, 4 * N], BF16, name="staged", bufs=4, align_bytes=64)
+                staged[unit] = work.tile([P, 4 * N], BF16, name="staged", bufs=10, align_bytes=256)
             words = staged[unit][:].bitcast(F32)[:, b * N:(b + 1) * N]
             nc.scalar.copy(
                 out=words.rearrange("p (s n u) -> p s n u", s=2, u=2),
@@ -147,11 +156,11 @@ def tile_groupedqueryattention_pa_kernel(
 
         def quantize(unit):
             depth = TOKEN_TILES if unit[0] == "x" else 2 * PASSES
-            codes[unit] = work.tile([P, N], U32, name=unit[0] + "_codes", bufs=depth, align_bytes=64)
-            scales[unit] = work.tile([P, N], U8, name=unit[0] + "_scales", bufs=depth, align_bytes=64)
+            codes[unit] = work.tile([P, N], U32, name=unit[0] + "_codes", bufs=depth, align_bytes=256)
+            scales[unit] = work.tile([P, N], U8, name=unit[0] + "_scales", bufs=depth, align_bytes=256)
             nc.vector.quantize_mx(out=codes[unit][:].bitcast(E5M2X4), scales=scales[unit][:], in_=staged[unit][:])
 
-        acc, stat, terms = {}, {}, {}
+        acc, stat, squares, terms, result = {}, {}, {}, {}, {}
 
         def multiply(group):
             c, m = group
@@ -168,15 +177,15 @@ def tile_groupedqueryattention_pa_kernel(
                     stop=(g == PASSES - 1),
                 )
 
-        def sum_squares(group):
-            stat[group] = work.tile([P, HEADS], F32, name="sums", bufs=3)
-            squares = work.tile([P, N], BF16, name="squares", bufs=2)
-            for h in range(HEADS):
-                cols = slice(h * D, (h + 1) * D)
-                nc.scalar.activation(
-                    out=squares[:, cols], in_=acc[group][:, cols], func=ACT.Square,
-                    accum_out=stat[group][:, h:h + 1],
-                )
+        def square_head(group, h):
+            if h == 0:
+                stat[group] = work.tile([P, HEADS], F32, name="sums", bufs=3)
+                squares[group] = work.tile([P, N], BF16, name="squares", bufs=2)
+            cols = slice(h * D, (h + 1) * D)
+            nc.scalar.activation(
+                out=squares[group][:, cols], in_=acc[group][:, cols], func=ACT.Square,
+                accum_out=stat[group][:, h:h + 1],
+            )
 
         def root(group):
             rms = work.tile([P, HEADS], F32, name="rms", bufs=3)
@@ -193,11 +202,12 @@ def tile_groupedqueryattention_pa_kernel(
             nc.vector.reciprocal(out=inverse[:], in_=stat[group][:])
             stat[group] = inverse
 
-        def products(group):
+        def products(group, heads):
             c, m = group
             table = tables[1 if c == K_CHUNK else 0]
-            terms[group] = work.tile([P, HEADS, 2, D], F32, name="terms", bufs=3)
-            for h in range(HEADS):
+            if group not in terms:
+                terms[group] = work.tile([P, HEADS, 2, D], F32, name="terms", bufs=4)
+            for h in heads:
                 nc.vector.scalar_tensor_tensor(
                     out=terms[group][:, h, :, :],
                     in0=acc[group][:, h * D:(h + 1) * D].unsqueeze(1).to_broadcast([P, 2, D]),
@@ -207,21 +217,37 @@ def tile_groupedqueryattention_pa_kernel(
                     op1=ALU.mult,
                 )
 
-        def rotate_and_store(group):
-            result = work.tile([P, HEADS, D], F32, name="result", bufs=12)
-            for lo, other in ((0, HALF), (HALF, 0)):
-                nc.vector.tensor_tensor(
-                    out=result[:, :, lo:lo + HALF],
-                    in0=terms[group][:, :, 0, lo:lo + HALF],
-                    in1=terms[group][:, :, 1, other:other + HALF],
-                    op=ALU.add,
-                )
-            nc.sync.dma_start(out=out_rows(*group), in_=result[:].rearrange("p h d -> p (h d)"))
+        def rotate_half(group, engine, lo):
+            other = HALF - lo
+            engine.tensor_tensor(
+                out=result[group].rearrange("p (h d) -> p h d", h=HEADS)[:, :, lo:lo + HALF],
+                in0=terms[group][:, :, 0, lo:lo + HALF],
+                in1=terms[group][:, :, 1, other:other + HALF],
+                op=ALU.add,
+            )
+
+        def first_half(group, unit):
+            if unit is None:
+                room = work.tile([P, N], F32, name="result", bufs=7)
+                result[group] = room[:]
+            else:
+                result[group] = staged[unit][:].bitcast(F32)[:, 0:N]
+            rotate_half(group, nc.gpsimd, 0)
+
+        def second_half(group):
+            rotate_half(group, nc.vector, HALF)
+            nc.sync.dma_start(out=out_rows(*group), in_=result[group])
+
+        def both_halves(group):
+            room = work.tile([P, N], F32, name="result", bufs=7)
+            result[group] = room[:]
+            rotate_half(group, nc.vector, 0)
+            second_half(group)
 
         def copy_and_store(group):
-            result = work.tile([P, N], F32, name="result", bufs=12)
-            nc.scalar.copy(out=result[:], in_=acc[group][:])
-            nc.sync.dma_start(out=out_rows(*group), in_=result[:])
+            room = work.tile([P, N], F32, name="result", bufs=7)
+            nc.scalar.copy(out=room[:], in_=acc[group][:])
+            nc.sync.dma_start(out=out_rows(*group), in_=room[:])
 
         for g in range(-1, PASSES):
             unit = ("x", 0) if g < 0 else ("w", 0, g)
@@ -238,41 +264,63 @@ def tile_groupedqueryattention_pa_kernel(
             for i in range(0, 4, 2):
                 steps += [([("w", c + 1, i + j) for j in range(2)], [(c, i + j) for j in range(2)])]
 
-        batch, waiting = [], []
+        normed = [(c, m) for c in range(V_CHUNK) for m in range(TOKEN_TILES)]
 
-        def finish(group):
+        def statistics(batch, copies):
+            for h in range(HEADS):
+                square_head(batch[0], h)
+            for first, group in zip(batch, batch[1:]):
+                square_head(group, 0)
+                square_head(group, 1)
+                root(first)
+                square_head(group, 2)
+                add_eps(first)
+                square_head(group, 3)
+            for call in (root, add_eps):
+                for unit, b in copies[:1]:
+                    empty_bank(unit, b)
+                copies = copies[1:]
+                call(batch[-1])
+            return copies
+
+        def vector_turn(group, to_sort, to_quantize):
+            place = normed.index(group)
+            for earlier in normed[max(place - 2, 0):max(place - 1, 0)]:
+                second_half(earlier)
+            for unit in to_sort:
+                sort_words(unit)
+            for unit in to_quantize[:-1]:
+                quantize(unit)
             invert(group)
-            for earlier in waiting:
-                rotate_and_store(earlier)
-            waiting.clear()
-            products(group)
-            waiting.append(group)
+            quantize(to_quantize[-1])
+            for earlier in normed[max(place - 1, 0):place]:
+                first_half(earlier, to_quantize[-1])
+            products(group, range(HEADS))
 
+        batch, deferred = [], []
         for number, (units, groups) in enumerate(steps):
+            for c, g in later[number:number + 1]:
+                load_w(c, g, 2)
             for unit in units:
                 transpose(unit)
-            for group in batch[:-1]:
-                sum_squares(group)
-                root(group)
-                add_eps(group)
             copies = [(unit, b) for unit in units for b in range(2)]
-            for group in batch[-1:]:
-                sum_squares(group)
-                empty_bank(*copies[0])
-                root(group)
-                empty_bank(*copies[1])
-                add_eps(group)
-                copies = copies[2:]
+            if batch:
+                copies = statistics(batch, copies)
             for unit, b in copies:
                 empty_bank(unit, b)
 
-            for group in batch[:-1]:
-                finish(group)
-            quantize(units[0])
-            for group in batch[-1:]:
-                finish(group)
-            for unit in units[1:]:
-                quantize(unit)
+            coming = steps[number + 1][0] if number + 1 < len(steps) else []
+            to_sort = [unit for unit in coming if unit[0] == "w" and unit[2] % 2 == 1]
+            if len(batch) == 2:
+                vector_turn(batch[0], to_sort, deferred)
+                vector_turn(batch[1], [], units[:1] if coming else units)
+            elif batch:
+                vector_turn(batch[0], to_sort, deferred + units[:1])
+            else:
+                quantize(units[0])
+                for unit in to_sort:
+                    sort_words(unit)
+            deferred = units[1:]
 
             for group in groups:
                 multiply(group)
@@ -281,14 +329,21 @@ def tile_groupedqueryattention_pa_kernel(
             batch = groups
 
         values = [(V_CHUNK, m) for m in range(TOKEN_TILES)]
+        statistics(batch, [])
+        second_half(normed[-4])
+        first_half(normed[-3], None)
+        invert(batch[0])
+        products(batch[0], range(0, HEADS - 1))
+        invert(batch[1])
+        products(batch[0], range(HEADS - 1, HEADS))
         for group in values:
             multiply(group)
-        for group in batch:
-            sum_squares(group)
-            root(group)
-            add_eps(group)
-            finish(group)
-        for group in values[:-1]:
-            copy_and_store(group)
-        rotate_and_store(waiting[0])
-        copy_and_store(values[-1])
+        copy_and_store(values[0])
+        copy_and_store(values[1])
+        second_half(normed[-3])
+        first_half(batch[0], None)
+        products(batch[1], range(HEADS))
+        copy_and_store(values[2])
+        second_half(batch[0])
+        copy_and_store(values[3])
+        both_halves(batch[1])

@@ -18,12 +18,19 @@ ALU = mybir.AluOpType
 
 P = 128
 N = 512
-PASSES = 4
-WORDS = 256
-TOKEN_TILES = 4
-HEADS = 4
-CHUNKS = 6
-K_CHUNK, V_CHUNK = 4, 5
+K_PASS = 512
+PASSES = C // K_PASS
+WORDS = K_PASS // 2
+SLOTS = 4
+TOKEN_TILES = T // P
+HEADS = N // D
+Q_CHUNKS, K_CHUNK, V_CHUNK = 4, 4, 5
+ALIGN = 256
+
+RAW_BUFS = 5
+STAGED_BUFS = 10
+TERM_BUFS = 4
+RESULT_BUFS = 7
 
 
 def tile_groupedqueryattention_pa_kernel(
@@ -31,8 +38,8 @@ def tile_groupedqueryattention_pa_kernel(
 ):
     nc = tc.nc
     x_rows = x[0].rearrange("(p m) k -> p m k", m=TOKEN_TILES)
-    w_rows = [Wq[c * N:(c + 1) * N, :] for c in range(4)] + [Wk, Wv]
-    w_rows = [w.rearrange("(r p) k -> p r k", p=P) for w in w_rows]
+    w_chunks = [Wq[c * N:(c + 1) * N, :] for c in range(Q_CHUNKS)] + [Wk, Wv]
+    w_rows = [w.rearrange("(r p) k -> p r k", p=P) for w in w_chunks]
     q_out = out_0[0].rearrange("(p m) h d -> p m (h d)", m=TOKEN_TILES)
     k_out = out_1[0].rearrange("(p m) h d -> p m (h d)", m=TOKEN_TILES)
     v_out = out_2[0].rearrange("(p m) h d -> p m (h d)", m=TOKEN_TILES)
@@ -53,30 +60,40 @@ def tile_groupedqueryattention_pa_kernel(
         ident = keep.tile([P, P], F32, name="ident")
         make_identity(nc, ident[:])
 
-        slots, packed, sorted_words = {}, {}, {}
+        slots, unit_words = {}, {}
 
         def load_x(m, pieces):
             slots[("x", m)] = []
             width = C // pieces
             for i in range(pieces):
-                raw = keep.tile([P, width], BF16, name="x_raw_%d_%d" % (m, i), align_bytes=256)
+                raw = keep.tile([P, width], BF16, name="x_raw_%d_%d" % (m, i), align_bytes=ALIGN)
                 nc.sync.dma_start(out=raw[:], in_=x_rows[:, m, i * width:(i + 1) * width])
                 words = raw[:].bitcast(F32)
                 for g in range(PASSES // pieces):
                     slots[("x", m)].append(words[:, g * WORDS:(g + 1) * WORDS])
 
-        def load_w(c, g0, count):
-            raw = work.tile([P, 4, count * 512], BF16, name="w_raw_%d" % count, bufs=5 if count == 2 else 4, align_bytes=256)
-            nc.sync.dma_start(out=raw[:], in_=w_rows[c][:, :, g0 * 512:(g0 + count) * 512])
+        def load_first_chunk(j):
+            half, pair = divmod(j, 2)
+            raw = keep.tile([P, 2, 2 * K_PASS], BF16, name="w_first_%d" % j, align_bytes=ALIGN)
+            nc.sync.dma_start(
+                out=raw[:], in_=w_rows[0][:, 2 * half:2 * half + 2, 2 * pair * K_PASS:2 * (pair + 1) * K_PASS]
+            )
             words = raw[:].bitcast(F32)
-            for j in range(count):
-                packed[("w", c, g0 + j)] = words[:, :, j * WORDS:(j + 1) * WORDS]
-                slots[("w", c, g0 + j)] = [words[:, r, j * WORDS:(j + 1) * WORDS] for r in range(4)]
+            slots[("w", 0, j)] = [words[:, r, g * WORDS:(g + 1) * WORDS] for g in range(2) for r in range(2)]
+
+        def load_w(c, first):
+            raw = work.tile([P, SLOTS, 2 * K_PASS], BF16, name="w_raw", bufs=RAW_BUFS, align_bytes=ALIGN)
+            nc.sync.dma_start(out=raw[:], in_=w_rows[c][:, :, first * K_PASS:(first + 2) * K_PASS])
+            words = raw[:].bitcast(F32)
+            for j in range(2):
+                unit_words[("w", c, first + j)] = words[:, :, j * WORDS:(j + 1) * WORDS]
+                slots[("w", c, first + j)] = [words[:, r, j * WORDS:(j + 1) * WORDS] for r in range(SLOTS)]
 
         load_x(0, 2)
-        for g in range(PASSES):
-            load_w(0, g, 1)
+        for j in range(4):
+            load_first_chunk(j)
         load_x(1, 1)
+
         gains = keep.tile([P, 2 * D], BF16, name="gains")
         ones = keep.tile([P, P], BF16, name="ones")
         nc.vector.memset(gains[:], 0.0)
@@ -89,29 +106,28 @@ def tile_groupedqueryattention_pa_kernel(
         nc.sync.dma_start(out=sin[:], in_=rope_sin.rearrange("(p m) i -> p m i", m=TOKEN_TILES))
 
         load_x(2, 1)
-        load_w(1, 0, 2)
+        load_w(1, 0)
         load_x(3, 1)
-        load_w(1, 2, 2)
-        later = [(c, g) for c in range(2, CHUNKS) for g in (0, 2)]
+        load_w(1, 2)
+        later_loads = [(c, first) for c in range(2, V_CHUNK + 1) for first in (0, 2)]
 
         tables = [keep.tile([P, TOKEN_TILES, 2, D], F32, name="table_%d" % i) for i in range(2)]
 
         def build_tables():
             spread = psum.tile([P, 2 * D], F32, name="spread", tag="acc")
             nc.tensor.matmul(spread[:], lhsT=ones[:], rhs=gains[:], start=True, stop=True)
+            both, one = [P, TOKEN_TILES, 2, HALF], [P, TOKEN_TILES, HALF]
             for i in range(2):
                 gain = spread[:, i * D:(i + 1) * D]
-                shape = [P, TOKEN_TILES, 2, HALF]
                 nc.vector.tensor_tensor(
                     out=tables[i][:, :, 0, :].rearrange("p m (a i) -> p m a i", a=2),
-                    in0=gain.rearrange("p (a i) -> p a i", a=2).unsqueeze(1).to_broadcast(shape),
-                    in1=cos[:].unsqueeze(2).to_broadcast(shape),
+                    in0=gain.rearrange("p (a i) -> p a i", a=2).unsqueeze(1).to_broadcast(both),
+                    in1=cos[:].unsqueeze(2).to_broadcast(both),
                     op=ALU.mult,
                 )
-                shape = [P, TOKEN_TILES, HALF]
                 nc.vector.scalar_tensor_tensor(
                     out=tables[i][:, :, 1, 0:HALF],
-                    in0=gain[:, 0:HALF].unsqueeze(1).to_broadcast(shape),
+                    in0=gain[:, 0:HALF].unsqueeze(1).to_broadcast(one),
                     scalar=-1.0,
                     in1=sin[:],
                     op0=ALU.mult,
@@ -119,18 +135,20 @@ def tile_groupedqueryattention_pa_kernel(
                 )
                 nc.vector.tensor_tensor(
                     out=tables[i][:, :, 1, HALF:D],
-                    in0=gain[:, HALF:D].unsqueeze(1).to_broadcast(shape),
+                    in0=gain[:, HALF:D].unsqueeze(1).to_broadcast(one),
                     in1=sin[:],
                     op=ALU.mult,
                 )
 
-        codes, scales, staged, banks = {}, {}, {}, {}
+        sorted_words, banks, staged, codes, scales = {}, {}, {}, {}, {}
 
-        def sort_words(unit):
-            sorted_words[unit] = work.tile([P, 2, 2, P], F32, name="sorted_words", bufs=3, align_bytes=256)
+        def sort_words(unit, first):
+            ordered = work.tile([P, SLOTS - first, 2, P], F32, name="ordered", bufs=3, align_bytes=ALIGN)
             nc.vector.tensor_copy(
-                out=sorted_words[unit][:], in_=packed[unit][:, 4 - 2:4, :].rearrange("p r (w u) -> p r u w", u=2)
+                out=ordered[:], in_=unit_words[unit][:, first:SLOTS, :].rearrange("p r (w u) -> p r u w", u=2)
             )
+            for s in range(first, SLOTS):
+                sorted_words[(unit, s)] = ordered[:, s - first, :, :]
 
         def transpose(unit):
             banks[unit] = []
@@ -138,8 +156,8 @@ def tile_groupedqueryattention_pa_kernel(
                 bank = psum.tile([P, 2, 2, P], F32, name="bank", tag="turn")
                 for s in range(2):
                     for u in range(2):
-                        if unit in sorted_words and 2 * b + s >= 4 - 2:
-                            source = sorted_words[unit][:, 2 * b + s - (4 - 2), u, :]
+                        if (unit, 2 * b + s) in sorted_words:
+                            source = sorted_words[(unit, 2 * b + s)][:, u, :]
                         else:
                             source = slots[unit][2 * b + s][:, u:WORDS:2]
                         nc.tensor.transpose(bank[:, s, u, :], source, ident[:])
@@ -147,7 +165,7 @@ def tile_groupedqueryattention_pa_kernel(
 
         def empty_bank(unit, b):
             if b == 0:
-                staged[unit] = work.tile([P, 4 * N], BF16, name="staged", bufs=10, align_bytes=256)
+                staged[unit] = work.tile([P, 4 * N], BF16, name="staged", bufs=STAGED_BUFS, align_bytes=ALIGN)
             words = staged[unit][:].bitcast(F32)[:, b * N:(b + 1) * N]
             nc.scalar.copy(
                 out=words.rearrange("p (s n u) -> p s n u", s=2, u=2),
@@ -156,8 +174,8 @@ def tile_groupedqueryattention_pa_kernel(
 
         def quantize(unit):
             depth = TOKEN_TILES if unit[0] == "x" else 2 * PASSES
-            codes[unit] = work.tile([P, N], U32, name=unit[0] + "_codes", bufs=depth, align_bytes=256)
-            scales[unit] = work.tile([P, N], U8, name=unit[0] + "_scales", bufs=depth, align_bytes=256)
+            codes[unit] = work.tile([P, N], U32, name=unit[0] + "_codes", bufs=depth, align_bytes=ALIGN)
+            scales[unit] = work.tile([P, N], U8, name=unit[0] + "_scales", bufs=depth, align_bytes=ALIGN)
             nc.vector.quantize_mx(out=codes[unit][:].bitcast(E5M2X4), scales=scales[unit][:], in_=staged[unit][:])
 
         acc, stat, squares, terms, result = {}, {}, {}, {}, {}
@@ -165,17 +183,24 @@ def tile_groupedqueryattention_pa_kernel(
         def multiply(group):
             c, m = group
             acc[group] = psum.tile([P, N], F32, name="acc", tag="turn" if c == V_CHUNK else "acc")
-            for g in range(PASSES):
-                cols = slice(g * P, (g + 1) * P)
-                nc.tensor.matmul_mx(
-                    out=acc[group][:],
-                    lhsT=codes[("x", m)][:, cols].bitcast(E5M2X4),
-                    lhsT_scale=scales[("x", m)][:, cols],
-                    rhs=codes[("w", c, g)][:].bitcast(E5M2X4),
-                    rhs_scale=scales[("w", c, g)][:],
-                    start=(g == 0),
-                    stop=(g == PASSES - 1),
-                )
+            parts = 2 if c == 0 else 1
+            width = N // parts
+            for part in range(parts):
+                for g in range(PASSES):
+                    tokens = slice(g * P, (g + 1) * P)
+                    if c == 0:
+                        unit, start = ("w", 0, 2 * part + g // 2), g % 2 * width
+                    else:
+                        unit, start = ("w", c, g), 0
+                    nc.tensor.matmul_mx(
+                        out=acc[group][:, part * width:(part + 1) * width],
+                        lhsT=codes[("x", m)][:, tokens].bitcast(E5M2X4),
+                        lhsT_scale=scales[("x", m)][:, tokens],
+                        rhs=codes[unit][:, start:start + width].bitcast(E5M2X4),
+                        rhs_scale=scales[unit][:, start:start + width],
+                        start=(g == 0),
+                        stop=(g == PASSES - 1),
+                    )
 
         def square_head(group, h):
             if h == 0:
@@ -206,7 +231,7 @@ def tile_groupedqueryattention_pa_kernel(
             c, m = group
             table = tables[1 if c == K_CHUNK else 0]
             if group not in terms:
-                terms[group] = work.tile([P, HEADS, 2, D], F32, name="terms", bufs=4)
+                terms[group] = work.tile([P, HEADS, 2, D], F32, name="terms", bufs=TERM_BUFS)
             for h in heads:
                 nc.vector.scalar_tensor_tensor(
                     out=terms[group][:, h, :, :],
@@ -226,34 +251,62 @@ def tile_groupedqueryattention_pa_kernel(
                 op=ALU.add,
             )
 
+        def new_result(group):
+            room = work.tile([P, N], F32, name="result", bufs=RESULT_BUFS)
+            result[group] = room[:]
+
         def first_half(group, unit):
-            if unit is None:
-                room = work.tile([P, N], F32, name="result", bufs=7)
-                result[group] = room[:]
-            else:
-                result[group] = staged[unit][:].bitcast(F32)[:, 0:N]
+            result[group] = staged[unit][:].bitcast(F32)[:, 0:N]
             rotate_half(group, nc.gpsimd, 0)
+
+        def store(group):
+            nc.sync.dma_start(out=out_rows(*group), in_=result[group])
 
         def second_half(group):
             rotate_half(group, nc.vector, HALF)
-            nc.sync.dma_start(out=out_rows(*group), in_=result[group])
+            store(group)
 
-        def both_halves(group):
-            room = work.tile([P, N], F32, name="result", bufs=7)
-            result[group] = room[:]
-            rotate_half(group, nc.vector, 0)
-            second_half(group)
+        def copy_values(group):
+            new_result(group)
+            nc.scalar.copy(out=result[group], in_=acc[group][:])
 
-        def copy_and_store(group):
-            room = work.tile([P, N], F32, name="result", bufs=7)
-            nc.scalar.copy(out=room[:], in_=acc[group][:])
-            nc.sync.dma_start(out=out_rows(*group), in_=room[:])
+        normed = [(c, m) for c in range(V_CHUNK) for m in range(TOKEN_TILES)]
 
-        for g in range(-1, PASSES):
-            unit = ("x", 0) if g < 0 else ("w", 0, g)
+        def scalar_turn(batch, units):
+            copies = [(unit, b) for unit in units for b in range(2)]
+            if batch:
+                for h in range(HEADS):
+                    square_head(batch[0], h)
+                for earlier, group in zip(batch, batch[1:]):
+                    root(earlier)
+                    square_head(group, 0)
+                    add_eps(earlier)
+                    for h in range(1, HEADS):
+                        square_head(group, h)
+                for call in (root, add_eps):
+                    for unit, b in copies[:1]:
+                        empty_bank(unit, b)
+                    copies = copies[1:]
+                    call(batch[-1])
+            for unit, b in copies:
+                empty_bank(unit, b)
+
+        def port_work(group, to_sort, to_quantize):
+            place = normed.index(group)
+            for earlier in normed[max(place - 2, 0):max(place - 1, 0)]:
+                second_half(earlier)
+            for unit, first in to_sort:
+                sort_words(unit, first)
+            for unit in to_quantize[:-1]:
+                quantize(unit)
+            invert(group)
+            quantize(to_quantize[-1])
+            for earlier in normed[max(place - 1, 0):place]:
+                first_half(earlier, to_quantize[-1])
+
+        for unit in [("x", 0)] + [("w", 0, j) for j in range(4)]:
             transpose(unit)
-            empty_bank(unit, 0)
-            empty_bank(unit, 1)
+            scalar_turn([], [unit])
             quantize(unit)
 
         steps = [([("x", 1)], [(0, 0)])]
@@ -261,65 +314,28 @@ def tile_groupedqueryattention_pa_kernel(
         steps += [([("x", 3), ("w", 1, 1)], [(0, 2)])]
         steps += [([("w", 1, 2), ("w", 1, 3)], [(0, 3)])]
         for c in range(1, V_CHUNK):
-            for i in range(0, 4, 2):
-                steps += [([("w", c + 1, i + j) for j in range(2)], [(c, i + j) for j in range(2)])]
-
-        normed = [(c, m) for c in range(V_CHUNK) for m in range(TOKEN_TILES)]
-
-        def statistics(batch, copies):
-            for h in range(HEADS):
-                square_head(batch[0], h)
-            for first, group in zip(batch, batch[1:]):
-                square_head(group, 0)
-                square_head(group, 1)
-                root(first)
-                square_head(group, 2)
-                add_eps(first)
-                square_head(group, 3)
-            for call in (root, add_eps):
-                for unit, b in copies[:1]:
-                    empty_bank(unit, b)
-                copies = copies[1:]
-                call(batch[-1])
-            return copies
-
-        def vector_turn(group, to_sort, to_quantize):
-            place = normed.index(group)
-            for earlier in normed[max(place - 2, 0):max(place - 1, 0)]:
-                second_half(earlier)
-            for unit in to_sort:
-                sort_words(unit)
-            for unit in to_quantize[:-1]:
-                quantize(unit)
-            invert(group)
-            quantize(to_quantize[-1])
-            for earlier in normed[max(place - 1, 0):place]:
-                first_half(earlier, to_quantize[-1])
-            products(group, range(HEADS))
+            for i in (0, 2):
+                steps += [([("w", c + 1, i), ("w", c + 1, i + 1)], [(c, i), (c, i + 1)])]
 
         batch, deferred = [], []
-        for number, (units, groups) in enumerate(steps):
-            for c, g in later[number:number + 1]:
-                load_w(c, g, 2)
+        for number, (units, groups) in enumerate(steps[:-1]):
+            for c, first in later_loads[number:number + 1]:
+                load_w(c, first)
             for unit in units:
                 transpose(unit)
-            copies = [(unit, b) for unit in units for b in range(2)]
-            if batch:
-                copies = statistics(batch, copies)
-            for unit, b in copies:
-                empty_bank(unit, b)
+            scalar_turn(batch, units)
 
-            coming = steps[number + 1][0] if number + 1 < len(steps) else []
-            to_sort = [unit for unit in coming if unit[0] == "w" and unit[2] % 2 == 1]
+            to_sort = [(steps[number + 1][0][1], 2 - number % 2)]
             if len(batch) == 2:
-                vector_turn(batch[0], to_sort, deferred)
-                vector_turn(batch[1], [], units[:1] if coming else units)
+                port_work(batch[0], to_sort, deferred)
+                products(batch[0], range(HEADS))
+                port_work(batch[1], [], units[:1])
+                products(batch[1], range(HEADS))
             elif batch:
-                vector_turn(batch[0], to_sort, deferred + units[:1])
+                port_work(batch[0], to_sort, deferred + units[:1])
+                products(batch[0], range(HEADS))
             else:
                 quantize(units[0])
-                for unit in to_sort:
-                    sort_words(unit)
             deferred = units[1:]
 
             for group in groups:
@@ -328,22 +344,35 @@ def tile_groupedqueryattention_pa_kernel(
                 build_tables()
             batch = groups
 
+        units, groups = steps[-1]
+        keys = batch + groups
         values = [(V_CHUNK, m) for m in range(TOKEN_TILES)]
-        statistics(batch, [])
-        second_half(normed[-4])
-        first_half(normed[-3], None)
-        invert(batch[0])
-        products(batch[0], range(0, HEADS - 1))
-        invert(batch[1])
-        products(batch[0], range(HEADS - 1, HEADS))
+        for unit in units:
+            transpose(unit)
+        scalar_turn(batch, units)
+        for group in groups:
+            multiply(group)
+        port_work(keys[0], [], deferred)
+        products(keys[0], range(HEADS))
+        port_work(keys[1], [], units)
         for group in values:
             multiply(group)
-        copy_and_store(values[0])
-        copy_and_store(values[1])
-        second_half(normed[-3])
-        first_half(batch[0], None)
-        products(batch[1], range(HEADS))
-        copy_and_store(values[2])
-        second_half(batch[0])
-        copy_and_store(values[3])
-        both_halves(batch[1])
+        scalar_turn(groups, [])
+        for group in values:
+            copy_values(group)
+
+        for i in (1, 2):
+            products(keys[i], range(HEADS - 1))
+            invert(keys[i + 1])
+            products(keys[i], [HEADS - 1])
+            second_half(keys[i - 1])
+            store(values[i - 1])
+            new_result(keys[i])
+            rotate_half(keys[i], nc.gpsimd, 0)
+        products(keys[3], range(HEADS))
+        store(values[2])
+        second_half(keys[2])
+        new_result(keys[3])
+        rotate_half(keys[3], nc.vector, 0)
+        second_half(keys[3])
+        store(values[3])

@@ -27,6 +27,8 @@ HEADS = N // D
 Q_CHUNKS, K_CHUNK, V_CHUNK = 4, 4, 5
 ALIGN = 256
 
+SORT_ALL_EVERY = 4
+
 RAW_BUFS = 5
 STAGED_BUFS = 10
 TERM_BUFS = 4
@@ -325,7 +327,7 @@ def tile_groupedqueryattention_pa_kernel(
                 transpose(unit)
             scalar_turn(batch, units)
 
-            to_sort = [(steps[number + 1][0][1], 2 - number % 2)]
+            to_sort = [(steps[number + 1][0][1], 0 if number % SORT_ALL_EVERY == 1 else 2)]
             if len(batch) == 2:
                 port_work(batch[0], to_sort, deferred)
                 products(batch[0], range(HEADS))

from contextlib import ExitStack

import concourse.mybir as mybir
from concourse.masks import make_identity

T, C, D = 512, 2048, 128
HALF = D // 2
EPS = 1e-6
FLOPS = 2 * T * C * (2048 + 512 + 512)

F32 = mybir.dt.float32
BF16 = mybir.dt.bfloat16
U32 = mybir.dt.uint32
U8 = mybir.dt.uint8
E5M2X4 = mybir.dt.float8_e5m2_x4
ACT = mybir.ActivationFunctionType
ALU = mybir.AluOpType

P = 128
N = 512
K_PASS = 512
PASSES = C // K_PASS
WORDS = K_PASS // 2
SLOTS = 4
TOKEN_TILES = T // P
HEADS = N // D
Q_CHUNKS, K_CHUNK, V_CHUNK = 4, 4, 5
ALIGN = 256

SORT_ALL_EVERY = 4

RAW_BUFS = 5
STAGED_BUFS = 10
TERM_BUFS = 4
RESULT_BUFS = 7


def tile_groupedqueryattention_pa_kernel(
    tc, x, Wq, Wk, Wv, q_norm_w, k_norm_w, rope_cos, rope_sin, out_0, out_1, out_2
):
    nc = tc.nc
    x_rows = x[0].rearrange("(p m) k -> p m k", m=TOKEN_TILES)
    w_chunks = [Wq[c * N:(c + 1) * N, :] for c in range(Q_CHUNKS)] + [Wk, Wv]
    w_rows = [w.rearrange("(r p) k -> p r k", p=P) for w in w_chunks]
    q_out = out_0[0].rearrange("(p m) h d -> p m (h d)", m=TOKEN_TILES)
    k_out = out_1[0].rearrange("(p m) h d -> p m (h d)", m=TOKEN_TILES)
    v_out = out_2[0].rearrange("(p m) h d -> p m (h d)", m=TOKEN_TILES)

    def out_rows(c, m):
        if c == K_CHUNK:
            return k_out[:, m, :]
        if c == V_CHUNK:
            return v_out[:, m, :]
        return q_out[:, m, c * N:(c + 1) * N]

    with ExitStack() as ctx:
        keep = ctx.enter_context(tc.tile_pool(name="keep", bufs=1))
        work = ctx.enter_context(tc.tile_pool(name="work", bufs=1))
        psum = ctx.enter_context(tc.psum_pool(name="psum", bufs=4))
        ctx.enter_context(tc.manual_schedule())

        ident = keep.tile([P, P], F32, name="ident")
        make_identity(nc, ident[:])

        slots, unit_words = {}, {}

        def load_x(m, pieces):
            slots[("x", m)] = []
            width = C // pieces
            for i in range(pieces):
                raw = keep.tile([P, width], BF16, name="x_raw_%d_%d" % (m, i), align_bytes=ALIGN)
                nc.sync.dma_start(out=raw[:], in_=x_rows[:, m, i * width:(i + 1) * width])
                words = raw[:].bitcast(F32)
                for g in range(PASSES // pieces):
                    slots[("x", m)].append(words[:, g * WORDS:(g + 1) * WORDS])

        def load_first_chunk(j):
            half, pair = divmod(j, 2)
            raw = keep.tile([P, 2, 2 * K_PASS], BF16, name="w_first_%d" % j, align_bytes=ALIGN)
            nc.sync.dma_start(
                out=raw[:], in_=w_rows[0][:, 2 * half:2 * half + 2, 2 * pair * K_PASS:2 * (pair + 1) * K_PASS]
            )
            words = raw[:].bitcast(F32)
            slots[("w", 0, j)] = [words[:, r, g * WORDS:(g + 1) * WORDS] for g in range(2) for r in range(2)]

        def load_w(c, first):
            raw = work.tile([P, SLOTS, 2 * K_PASS], BF16, name="w_raw", bufs=RAW_BUFS, align_bytes=ALIGN)
            nc.sync.dma_start(out=raw[:], in_=w_rows[c][:, :, first * K_PASS:(first + 2) * K_PASS])
            words = raw[:].bitcast(F32)
            for j in range(2):
                unit_words[("w", c, first + j)] = words[:, :, j * WORDS:(j + 1) * WORDS]
                slots[("w", c, first + j)] = [words[:, r, j * WORDS:(j + 1) * WORDS] for r in range(SLOTS)]

        load_x(0, 2)
        for j in range(4):
            load_first_chunk(j)
        load_x(1, 1)

        gains = keep.tile([P, 2 * D], BF16, name="gains")
        ones = keep.tile([P, P], BF16, name="ones")
        nc.vector.memset(gains[:], 0.0)
        nc.vector.memset(ones[:], 1.0)
        cos = keep.tile([P, TOKEN_TILES, HALF], BF16, name="cos")
        sin = keep.tile([P, TOKEN_TILES, HALF], BF16, name="sin")
        nc.sync.dma_start(out=gains[0:1, 0:D], in_=q_norm_w.unsqueeze(0))
        nc.sync.dma_start(out=gains[0:1, D:2 * D], in_=k_norm_w.unsqueeze(0))
        nc.sync.dma_start(out=cos[:], in_=rope_cos.rearrange("(p m) i -> p m i", m=TOKEN_TILES))
        nc.sync.dma_start(out=sin[:], in_=rope_sin.rearrange("(p m) i -> p m i", m=TOKEN_TILES))

        load_x(2, 1)
        load_w(1, 0)
        load_x(3, 1)
        load_w(1, 2)
        later_loads = [(c, first) for c in range(2, V_CHUNK + 1) for first in (0, 2)]

        tables = [keep.tile([P, TOKEN_TILES, 2, D], F32, name="table_%d" % i) for i in range(2)]

        def build_tables():
            spread = psum.tile([P, 2 * D], F32, name="spread", tag="acc")
            nc.tensor.matmul(spread[:], lhsT=ones[:], rhs=gains[:], start=True, stop=True)
            both, one = [P, TOKEN_TILES, 2, HALF], [P, TOKEN_TILES, HALF]
            for i in range(2):
                gain = spread[:, i * D:(i + 1) * D]
                nc.vector.tensor_tensor(
                    out=tables[i][:, :, 0, :].rearrange("p m (a i) -> p m a i", a=2),
                    in0=gain.rearrange("p (a i) -> p a i", a=2).unsqueeze(1).to_broadcast(both),
                    in1=cos[:].unsqueeze(2).to_broadcast(both),
                    op=ALU.mult,
                )
                nc.vector.scalar_tensor_tensor(
                    out=tables[i][:, :, 1, 0:HALF],
                    in0=gain[:, 0:HALF].unsqueeze(1).to_broadcast(one),
                    scalar=-1.0,
                    in1=sin[:],
                    op0=ALU.mult,
                    op1=ALU.mult,
                )
                nc.vector.tensor_tensor(
                    out=tables[i][:, :, 1, HALF:D],
                    in0=gain[:, HALF:D].unsqueeze(1).to_broadcast(one),
                    in1=sin[:],
                    op=ALU.mult,
                )

        sorted_words, banks, staged, codes, scales = {}, {}, {}, {}, {}

        def sort_words(unit, first):
            ordered = work.tile([P, SLOTS - first, 2, P], F32, name="ordered", bufs=3, align_bytes=ALIGN)
            nc.vector.tensor_copy(
                out=ordered[:], in_=unit_words[unit][:, first:SLOTS, :].rearrange("p r (w u) -> p r u w", u=2)
            )
            for s in range(first, SLOTS):
                sorted_words[(unit, s)] = ordered[:, s - first, :, :]

        def transpose(unit):
            banks[unit] = []
            for b in range(2):
                bank = psum.tile([P, 2, 2, P], F32, name="bank", tag="turn")
                for s in range(2):
                    for u in range(2):
                        if (unit, 2 * b + s) in sorted_words:
                            source = sorted_words[(unit, 2 * b + s)][:, u, :]
                        else:
                            source = slots[unit][2 * b + s][:, u:WORDS:2]
                        nc.tensor.transpose(bank[:, s, u, :], source, ident[:])
                banks[unit].append(bank)

        def empty_bank(unit, b):
            if b == 0:
                staged[unit] = work.tile([P, 4 * N], BF16, name="staged", bufs=STAGED_BUFS, align_bytes=ALIGN)
            words = staged[unit][:].bitcast(F32)[:, b * N:(b + 1) * N]
            nc.scalar.copy(
                out=words.rearrange("p (s n u) -> p s n u", s=2, u=2),
                in_=banks[unit][b][:].rearrange("p s u n -> p s n u"),
            )

        def quantize(unit):
            depth = TOKEN_TILES if unit[0] == "x" else 2 * PASSES
            codes[unit] = work.tile([P, N], U32, name=unit[0] + "_codes", bufs=depth, align_bytes=ALIGN)
            scales[unit] = work.tile([P, N], U8, name=unit[0] + "_scales", bufs=depth, align_bytes=ALIGN)
            nc.vector.quantize_mx(out=codes[unit][:].bitcast(E5M2X4), scales=scales[unit][:], in_=staged[unit][:])

        acc, stat, squares, terms, result = {}, {}, {}, {}, {}

        def multiply(group):
            c, m = group
            acc[group] = psum.tile([P, N], F32, name="acc", tag="turn" if c == V_CHUNK else "acc")
            parts = 2 if c == 0 else 1
            width = N // parts
            for part in range(parts):
                for g in range(PASSES):
                    tokens = slice(g * P, (g + 1) * P)
                    if c == 0:
                        unit, start = ("w", 0, 2 * part + g // 2), g % 2 * width
                    else:
                        unit, start = ("w", c, g), 0
                    nc.tensor.matmul_mx(
                        out=acc[group][:, part * width:(part + 1) * width],
                        lhsT=codes[("x", m)][:, tokens].bitcast(E5M2X4),
                        lhsT_scale=scales[("x", m)][:, tokens],
                        rhs=codes[unit][:, start:start + width].bitcast(E5M2X4),
                        rhs_scale=scales[unit][:, start:start + width],
                        start=(g == 0),
                        stop=(g == PASSES - 1),
                    )

        def square_head(group, h):
            if h == 0:
                stat[group] = work.tile([P, HEADS], F32, name="sums", bufs=3)
                squares[group] = work.tile([P, N], BF16, name="squares", bufs=2)
            cols = slice(h * D, (h + 1) * D)
            nc.scalar.activation(
                out=squares[group][:, cols], in_=acc[group][:, cols], func=ACT.Square,
                accum_out=stat[group][:, h:h + 1],
            )

        def root(group):
            rms = work.tile([P, HEADS], F32, name="rms", bufs=3)
            nc.scalar.activation(out=rms[:], in_=stat[group][:], func=ACT.Sqrt, scale=1.0 / D)
            stat[group] = rms

        def add_eps(group):
            padded = work.tile([P, HEADS], F32, name="padded", bufs=3)
            nc.scalar.activation(out=padded[:], in_=stat[group][:], func=ACT.Copy, bias=EPS)
            stat[group] = padded

        def invert(group):
            inverse = work.tile([P, HEADS], F32, name="inverse", bufs=3)
            nc.vector.reciprocal(out=inverse[:], in_=stat[group][:])
            stat[group] = inverse

        def products(group, heads):
            c, m = group
            table = tables[1 if c == K_CHUNK else 0]
            if group not in terms:
                terms[group] = work.tile([P, HEADS, 2, D], F32, name="terms", bufs=TERM_BUFS)
            for h in heads:
                nc.vector.scalar_tensor_tensor(
                    out=terms[group][:, h, :, :],
                    in0=acc[group][:, h * D:(h + 1) * D].unsqueeze(1).to_broadcast([P, 2, D]),
                    scalar=stat[group][:, h:h + 1],
                    in1=table[:, m, :, :],
                    op0=ALU.mult,
                    op1=ALU.mult,
                )

        def rotate_half(group, engine, lo):
            other = HALF - lo
            engine.tensor_tensor(
                out=result[group].rearrange("p (h d) -> p h d", h=HEADS)[:, :, lo:lo + HALF],
                in0=terms[group][:, :, 0, lo:lo + HALF],
                in1=terms[group][:, :, 1, other:other + HALF],
                op=ALU.add,
            )

        def new_result(group):
            room = work.tile([P, N], F32, name="result", bufs=RESULT_BUFS)
            result[group] = room[:]

        def first_half(group, unit):
            result[group] = staged[unit][:].bitcast(F32)[:, 0:N]
            rotate_half(group, nc.gpsimd, 0)

        def store(group):
            nc.sync.dma_start(out=out_rows(*group), in_=result[group])

        def second_half(group):
            rotate_half(group, nc.vector, HALF)
            store(group)

        def copy_values(group):
            new_result(group)
            nc.scalar.copy(out=result[group], in_=acc[group][:])

        normed = [(c, m) for c in range(V_CHUNK) for m in range(TOKEN_TILES)]

        def scalar_turn(batch, units):
            copies = [(unit, b) for unit in units for b in range(2)]
            if batch:
                for h in range(HEADS):
                    square_head(batch[0], h)
                for earlier, group in zip(batch, batch[1:]):
                    root(earlier)
                    square_head(group, 0)
                    add_eps(earlier)
                    for h in range(1, HEADS):
                        square_head(group, h)
                for call in (root, add_eps):
                    for unit, b in copies[:1]:
                        empty_bank(unit, b)
                    copies = copies[1:]
                    call(batch[-1])
            for unit, b in copies:
                empty_bank(unit, b)

        def port_work(group, to_sort, to_quantize):
            place = normed.index(group)
            for earlier in normed[max(place - 2, 0):max(place - 1, 0)]:
                second_half(earlier)
            for unit, first in to_sort:
                sort_words(unit, first)
            for unit in to_quantize[:-1]:
                quantize(unit)
            invert(group)
            quantize(to_quantize[-1])
            for earlier in normed[max(place - 1, 0):place]:
                first_half(earlier, to_quantize[-1])

        for unit in [("x", 0)] + [("w", 0, j) for j in range(4)]:
            transpose(unit)
            scalar_turn([], [unit])
            quantize(unit)

        steps = [([("x", 1)], [(0, 0)])]
        steps += [([("x", 2), ("w", 1, 0)], [(0, 1)])]
        steps += [([("x", 3), ("w", 1, 1)], [(0, 2)])]
        steps += [([("w", 1, 2), ("w", 1, 3)], [(0, 3)])]
        for c in range(1, V_CHUNK):
            for i in (0, 2):
                steps += [([("w", c + 1, i), ("w", c + 1, i + 1)], [(c, i), (c, i + 1)])]

        batch, deferred = [], []
        for number, (units, groups) in enumerate(steps[:-1]):
            for c, first in later_loads[number:number + 1]:
                load_w(c, first)
            for unit in units:
                transpose(unit)
            scalar_turn(batch, units)

            to_sort = [(steps[number + 1][0][1], 0 if number % SORT_ALL_EVERY == 1 else 2)]
            if len(batch) == 2:
                port_work(batch[0], to_sort, deferred)
                products(batch[0], range(HEADS))
                port_work(batch[1], [], units[:1])
                products(batch[1], range(HEADS))
            elif batch:
                port_work(batch[0], to_sort, deferred + units[:1])
                products(batch[0], range(HEADS))
            else:
                quantize(units[0])
            deferred = units[1:]

            for group in groups:
                multiply(group)
            if number == 0:
                build_tables()
            batch = groups

        units, groups = steps[-1]
        keys = batch + groups
        values = [(V_CHUNK, m) for m in range(TOKEN_TILES)]
        for unit in units:
            transpose(unit)
        scalar_turn(batch, units)
        for group in groups:
            multiply(group)
        port_work(keys[0], [], deferred)
        products(keys[0], range(HEADS))
        port_work(keys[1], [], units)
        for group in values:
            multiply(group)
        scalar_turn(groups, [])
        for group in values:
            copy_values(group)

        for i in (1, 2):
            products(keys[i], range(HEADS - 1))
            invert(keys[i + 1])
            products(keys[i], [HEADS - 1])
            second_half(keys[i - 1])
            store(values[i - 1])
            new_result(keys[i])
            rotate_half(keys[i], nc.gpsimd, 0)
        products(keys[3], range(HEADS))
        store(values[2])
        second_half(keys[2])
        new_result(keys[3])
        rotate_half(keys[3], nc.vector, 0)
        second_half(keys[3])
        store(values[3])
